import numpy as np
import ml_dtypes


def mxq(x, axis, fmt="e4m3"):
    dtype, down = {"e4m3": (ml_dtypes.float8_e4m3fn, 7), "e5m2": (ml_dtypes.float8_e5m2, 14)}[fmt]
    v = np.moveaxis(np.asarray(x, np.float32).astype(ml_dtypes.bfloat16).astype(np.float64), axis, -1)
    blocks = v.reshape(v.shape[:-1] + (-1, 32))
    amax = np.abs(blocks).max(-1, keepdims=True)
    byte = np.maximum(np.where(amax > 0, np.frexp(amax)[1] - 1 + 127, 0) - down, 1)
    scale = np.exp2(byte - 127.0)
    codes = (blocks / scale).astype(np.float32).astype(dtype).astype(np.float64)
    return np.moveaxis((codes * scale).reshape(v.shape), -1, axis)


WIDE = False


def mx_kscale(k):
    if not WIDE:
        return np.ones(k)
    levels = np.array([10, -10, 5, -5, 0])
    if k % 512:
        return np.exp2(np.random.permutation(np.resize(levels, k // 32))).repeat(32)
    a = np.empty((k // 512, 16))
    for p in range(k // 512):
        a[p, :8] = np.random.permutation(np.resize(levels, 8))
        for g in range(8):
            far = levels[np.abs(levels - a[p, g]) >= 10]
            a[p, g + 8] = far[np.random.randint(len(far))]
    return np.exp2(a.ravel()).repeat(32)


BF16 = ml_dtypes.bfloat16


def bf(x):
    return np.asarray(x, np.float32).astype(BF16)


def f64(x):
    return np.asarray(x).astype(np.float64)


B, D, I, O = 1024, 8, 512, 256


def setup_inputs():
    s = np.tile(mx_kscale(I), D)
    return {"x": bf(np.random.standard_normal((B, D * I)) * s),
            "W": bf(np.random.standard_normal((D * O, D * I)) / np.sqrt(I) / s[None, :])}


def reference(x, W):
    W4 = f64(W).reshape(D, O, D, I)
    Wb = np.ascontiguousarray(np.einsum('dodi->doi', W4))
    xb = f64(x).reshape(B, D, I)
    xq = mxq(xb, 2, "e4m3")
    wq = mxq(Wb, 2, "e4m3")
    out = xq.transpose(1, 0, 2) @ wq.transpose(0, 2, 1)
    return out.transpose(1, 0, 2).reshape(B, D * O)

@@ -1,0 +1,123 @@
+from contextlib import ExitStack
+
+import concourse.mybir as mybir
+from concourse.masks import make_identity
+
+F32 = mybir.dt.float32
+BF16 = mybir.dt.bfloat16
+U32 = mybir.dt.uint32
+U8 = mybir.dt.uint8
+FP8X4 = mybir.dt.float8_e4m3fn_x4
+
+P = 128
+B, D, I, O = 1024, 8, 512, 256
+NT = B // P
+FLOPS = 2 * B * D * I * O
+BYTES = B * D * I * 2 + D * O * I * 2 + B * D * O * 4
+
+PIN = True
+
+
+def tile_ensemblelinear_kernel(tc, x, W, out):
+    nc = tc.nc
+    with ExitStack() as ctx:
+        keep = ctx.enter_context(tc.tile_pool(name="keep", bufs=1))
+        xpool = ctx.enter_context(tc.tile_pool(name="xpool", bufs=NT))
+        wpool = ctx.enter_context(tc.tile_pool(name="wpool", bufs=D))
+        gpool = ctx.enter_context(tc.tile_pool(name="gpool", bufs=3))
+        opool = ctx.enter_context(tc.tile_pool(name="opool", bufs=NT))
+        tps = ctx.enter_context(tc.psum_pool(name="tps", bufs=4))
+        aps = ctx.enter_context(tc.psum_pool(name="aps", bufs=4))
+        if PIN:
+            ctx.enter_context(tc.manual_schedule())
+
+        x_v = x.rearrange("(p t) k -> p t k", t=NT)
+        out_v = out.rearrange("(p t) n -> p t n", t=NT)
+
+        w_sb = []
+        for d in range(D):
+            wt = wpool.tile([P, 2 * I], BF16, name="w_raw", tag="w_raw")
+            nc.sync.dma_start(
+                out=wt[:].rearrange("p (h k) -> p h k", h=2),
+                in_=W[O * d : O * (d + 1), I * d : I * (d + 1)].rearrange("(h p) k -> p h k", p=P),
+            )
+            w_sb.append(wt)
+        x_sb = []
+        for i in range(NT):
+            xt = xpool.tile([P, D * I], BF16, name="x_raw", tag="x_raw")
+            nc.sync.dma_start(out=xt[:], in_=x_v[:, i, :])
+            x_sb.append(xt)
+
+        ident = keep.tile([P, P], F32, name="ident")
+        make_identity(nc, ident[:])
+
+        def flip(src_words, first_word, dst_bf16, engine):
+            bank = tps.tile([P, 2, 2 * P], F32, name="flip_bank", tag="flip_bank")
+            for c in range(2):
+                for u in range(2):
+                    col = first_word + 2 * P * c
+                    nc.tensor.transpose(bank[:, u, P * c : P * (c + 1)], src_words[:, col + u : col + 2 * P : 2], ident[:])
+            dst = dst_bf16.bitcast(F32).rearrange("p (c u) -> p c u", u=2)
+            src = bank[:].rearrange("p u c -> p c u")
+            if engine == "v":
+                nc.vector.tensor_copy(out=dst, in_=src)
+            else:
+                nc.scalar.copy(out=dst, in_=src)
+
+        w_grp, w_codes, w_scales = [], [], []
+        for j in range(D // 2):
+            w_grp.append(keep.tile([P, 2048], BF16, name="w_grp%d" % j, align_bytes=64))
+            w_codes.append(keep.tile([P, 512], U32, name="w_codes%d" % j, align_bytes=64))
+            w_scales.append(keep.tile([P, 512], U8, name="w_scales%d" % j, align_bytes=64))
+
+        def quant_w(j):
+            nc.vector.quantize_mx(out=w_codes[j][:].bitcast(FP8X4), scales=w_scales[j][:], in_=w_grp[j][:])
+
+        for d in range(D):
+            j, dd = d // 2, d % 2
+            flip(w_sb[d][:].bitcast(F32), 0, w_grp[j][:, 1024 * dd : 1024 * (dd + 1)], "s" if dd == 0 else "v")
+            if dd == 1 and j >= 1:
+                quant_w(j - 1)
+        quant_w(D // 2 - 1)
+
+        grp, codes, scales = {}, {}, {}
+
+        def flip_x(i):
+            grp[i] = gpool.tile([P, D * I], BF16, name="x_grp", tag="x_grp", align_bytes=64)
+            xw = x_sb[i][:].bitcast(F32)
+            for j in range(4):
+                flip(xw, 512 * j, grp[i][:, 1024 * j : 1024 * (j + 1)], "v" if j == 3 else "s")
+
+        def quant_x(i):
+            codes[i] = gpool.tile([P, D * P], U32, name="x_codes", tag="x_codes", align_bytes=64)
+            scales[i] = gpool.tile([P, D * P], U8, name="x_scales", tag="x_scales", align_bytes=64)
+            nc.vector.quantize_mx(out=codes[i][:].bitcast(FP8X4), scales=scales[i][:], in_=grp[i][:])
+
+        def multiply(i):
+            res = opool.tile([P, D * O], F32, name="res", tag="res")
+            for j in range(4):
+                acc = aps.tile([P, 2 * O], F32, name="acc", tag="acc")
+                for dd in range(2):
+                    d = 2 * j + dd
+                    nc.tensor.matmul_mx(
+                        out=acc[:, O * dd : O * (dd + 1)],
+                        lhsT=codes[i][:, P * d : P * (d + 1)].bitcast(FP8X4),
+                        lhsT_scale=scales[i][:, P * d : P * (d + 1)],
+                        rhs=w_codes[j][:, O * dd : O * (dd + 1)].bitcast(FP8X4),
+                        rhs_scale=w_scales[j][:, O * dd : O * (dd + 1)],
+                        start=True,
+                        stop=True,
+                    )
+                dst = res[:, 512 * j : 512 * (j + 1)]
+                if j % 2 == 0:
+                    nc.vector.tensor_copy(out=dst, in_=acc[:])
+                else:
+                    nc.scalar.copy(out=dst, in_=acc[:])
+            nc.sync.dma_start(out=out_v[:, i, :], in_=res[:])
+
+        flip_x(0)
+        for i in range(NT):
+            quant_x(i)
+            if i + 1 < NT:
+                flip_x(i + 1)
+            multiply(i)

@@ -75,7 +75,7 @@ def tile_ensemblelinear_kernel(tc, x, W, out):
 
         for d in range(D):
             j, dd = d // 2, d % 2
-            flip(w_sb[d][:].bitcast(F32), 0, w_grp[j][:, 1024 * dd : 1024 * (dd + 1)], "s" if dd == 0 else "v")
+            flip(w_sb[d][:].bitcast(F32), 0, w_grp[j][:, 1024 * dd : 1024 * (dd + 1)], "v" if d % 4 == 2 else "s")
             if dd == 1 and j >= 1:
                 quant_w(j - 1)
         quant_w(D // 2 - 1)
@@ -86,7 +86,7 @@ def tile_ensemblelinear_kernel(tc, x, W, out):
             grp[i] = gpool.tile([P, D * I], BF16, name="x_grp", tag="x_grp", align_bytes=64)
             xw = x_sb[i][:].bitcast(F32)
             for j in range(4):
-                flip(xw, 512 * j, grp[i][:, 1024 * j : 1024 * (j + 1)], "v" if j == 3 else "s")
+                flip(xw, 512 * j, grp[i][:, 1024 * j : 1024 * (j + 1)], "v" if j == 1 else "s")
 
         def quant_x(i):
             codes[i] = gpool.tile([P, D * P], U32, name="x_codes", tag="x_codes", align_bytes=64)
@@ -111,13 +111,15 @@ def tile_ensemblelinear_kernel(tc, x, W, out):
                 dst = res[:, 512 * j : 512 * (j + 1)]
                 if j % 2 == 0:
                     nc.vector.tensor_copy(out=dst, in_=acc[:])
+                    if j == 0 and i + 1 < NT:
+                        quant_x(i + 1)
                 else:
                     nc.scalar.copy(out=dst, in_=acc[:])
             nc.sync.dma_start(out=out_v[:, i, :], in_=res[:])
 
         flip_x(0)
+        quant_x(0)
         for i in range(NT):
-            quant_x(i)
             if i + 1 < NT:
                 flip_x(i + 1)
             multiply(i)

@@ -31,8 +31,8 @@ def tile_ensemblelinear_kernel(tc, x, W, out):
         if PIN:
             ctx.enter_context(tc.manual_schedule())
 
-        x_v = x.rearrange("(p t) k -> p t k", t=NT)
-        out_v = out.rearrange("(p t) n -> p t n", t=NT)
+        x_v = x.rearrange("(t p) k -> p t k", t=NT)
+        out_v = out.rearrange("(t p) n -> p t n", t=NT)
 
         w_sb = []
         for d in range(D):

@@ -24,7 +24,7 @@ def tile_ensemblelinear_kernel(tc, x, W, out):
         keep = ctx.enter_context(tc.tile_pool(name="keep", bufs=1))
         xpool = ctx.enter_context(tc.tile_pool(name="xpool", bufs=NT))
         wpool = ctx.enter_context(tc.tile_pool(name="wpool", bufs=D))
-        gpool = ctx.enter_context(tc.tile_pool(name="gpool", bufs=3))
+        gpool = ctx.enter_context(tc.tile_pool(name="gpool", bufs=4))
         opool = ctx.enter_context(tc.tile_pool(name="opool", bufs=NT))
         tps = ctx.enter_context(tc.psum_pool(name="tps", bufs=4))
         aps = ctx.enter_context(tc.psum_pool(name="aps", bufs=4))
@@ -80,46 +80,54 @@ def tile_ensemblelinear_kernel(tc, x, W, out):
                 quant_w(j - 1)
         quant_w(D // 2 - 1)
 
-        grp, codes, scales = {}, {}, {}
+        grp, codes, scales, res = {}, {}, {}, {}
+        NU = 2 * NT
 
-        def flip_x(i):
-            grp[i] = gpool.tile([P, D * I], BF16, name="x_grp", tag="x_grp", align_bytes=64)
+        def flip_x(u):
+            i, h = u // 2, u % 2
+            grp[u] = gpool.tile([P, 2048], BF16, name="x_grp", tag="x_grp", align_bytes=64)
             xw = x_sb[i][:].bitcast(F32)
-            for j in range(4):
-                flip(xw, 512 * j, grp[i][:, 1024 * j : 1024 * (j + 1)], "v" if j == 1 else "s")
+            for j in range(2):
+                on_vector = j == 1 and h == 0
+                flip(xw, 1024 * h + 512 * j, grp[u][:, 1024 * j : 1024 * (j + 1)], "v" if on_vector else "s")
 
-        def quant_x(i):
-            codes[i] = gpool.tile([P, D * P], U32, name="x_codes", tag="x_codes", align_bytes=64)
-            scales[i] = gpool.tile([P, D * P], U8, name="x_scales", tag="x_scales", align_bytes=64)
-            nc.vector.quantize_mx(out=codes[i][:].bitcast(FP8X4), scales=scales[i][:], in_=grp[i][:])
+        def quant_x(u):
+            codes[u] = gpool.tile([P, 4 * P], U32, name="x_codes", tag="x_codes", align_bytes=64)
+            scales[u] = gpool.tile([P, 4 * P], U8, name="x_scales", tag="x_scales", align_bytes=64)
+            nc.vector.quantize_mx(out=codes[u][:].bitcast(FP8X4), scales=scales[u][:], in_=grp[u][:])
 
-        def multiply(i):
-            res = opool.tile([P, D * O], F32, name="res", tag="res")
-            for j in range(4):
+        def multiply(u):
+            i, h = u // 2, u % 2
+            if h == 0:
+                res[i] = opool.tile([P, D * O], F32, name="res", tag="res")
+            for jj in range(2):
+                j = 2 * h + jj
                 acc = aps.tile([P, 2 * O], F32, name="acc", tag="acc")
                 for dd in range(2):
-                    d = 2 * j + dd
+                    dl = 2 * jj + dd
                     nc.tensor.matmul_mx(
                         out=acc[:, O * dd : O * (dd + 1)],
-                        lhsT=codes[i][:, P * d : P * (d + 1)].bitcast(FP8X4),
-                        lhsT_scale=scales[i][:, P * d : P * (d + 1)],
+                        lhsT=codes[u][:, P * dl : P * (dl + 1)].bitcast(FP8X4),
+                        lhsT_scale=scales[u][:, P * dl : P * (dl + 1)],
                         rhs=w_codes[j][:, O * dd : O * (dd + 1)].bitcast(FP8X4),
                         rhs_scale=w_scales[j][:, O * dd : O * (dd + 1)],
                         start=True,
                         stop=True,
                     )
-                dst = res[:, 512 * j : 512 * (j + 1)]
-                if j % 2 == 0:
+                dst = res[i][:, 512 * j : 512 * (j + 1)]
+                if jj == 0:
                     nc.vector.tensor_copy(out=dst, in_=acc[:])
-                    if j == 0 and i + 1 < NT:
-                        quant_x(i + 1)
                 else:
                     nc.scalar.copy(out=dst, in_=acc[:])
-            nc.sync.dma_start(out=out_v[:, i, :], in_=res[:])
+            if h == 1:
+                nc.sync.dma_start(out=out_v[:, i, :], in_=res[i][:])
 
         flip_x(0)
+        flip_x(1)
         quant_x(0)
-        for i in range(NT):
-            if i + 1 < NT:
-                flip_x(i + 1)
-            multiply(i)
+        for u in range(NU):
+            if u + 1 < NU:
+                quant_x(u + 1)
+            if u + 2 < NU:
+                flip_x(u + 2)
+            multiply(u)

from contextlib import ExitStack

import concourse.mybir as mybir
from concourse.masks import make_identity

F32 = mybir.dt.float32
BF16 = mybir.dt.bfloat16
U32 = mybir.dt.uint32
U8 = mybir.dt.uint8
FP8X4 = mybir.dt.float8_e4m3fn_x4

P = 128
B, D, I, O = 1024, 8, 512, 256
NT = B // P
FLOPS = 2 * B * D * I * O
BYTES = B * D * I * 2 + D * O * I * 2 + B * D * O * 4

PIN = True


def tile_ensemblelinear_kernel(tc, x, W, out):
    nc = tc.nc
    with ExitStack() as ctx:
        keep = ctx.enter_context(tc.tile_pool(name="keep", bufs=1))
        xpool = ctx.enter_context(tc.tile_pool(name="xpool", bufs=NT))
        wpool = ctx.enter_context(tc.tile_pool(name="wpool", bufs=D))
        gpool = ctx.enter_context(tc.tile_pool(name="gpool", bufs=4))
        opool = ctx.enter_context(tc.tile_pool(name="opool", bufs=NT))
        tps = ctx.enter_context(tc.psum_pool(name="tps", bufs=4))
        aps = ctx.enter_context(tc.psum_pool(name="aps", bufs=4))
        if PIN:
            ctx.enter_context(tc.manual_schedule())

        x_v = x.rearrange("(t p) k -> p t k", t=NT)
        out_v = out.rearrange("(t p) n -> p t n", t=NT)

        w_sb = []
        for d in range(D):
            wt = wpool.tile([P, 2 * I], BF16, name="w_raw", tag="w_raw")
            nc.sync.dma_start(
                out=wt[:].rearrange("p (h k) -> p h k", h=2),
                in_=W[O * d : O * (d + 1), I * d : I * (d + 1)].rearrange("(h p) k -> p h k", p=P),
            )
            w_sb.append(wt)
        x_sb = []
        for i in range(NT):
            xt = xpool.tile([P, D * I], BF16, name="x_raw", tag="x_raw")
            nc.sync.dma_start(out=xt[:], in_=x_v[:, i, :])
            x_sb.append(xt)

        ident = keep.tile([P, P], F32, name="ident")
        make_identity(nc, ident[:])

        def flip(src_words, first_word, dst_bf16, engine):
            bank = tps.tile([P, 2, 2 * P], F32, name="flip_bank", tag="flip_bank")
            for c in range(2):
                for u in range(2):
                    col = first_word + 2 * P * c
                    nc.tensor.transpose(bank[:, u, P * c : P * (c + 1)], src_words[:, col + u : col + 2 * P : 2], ident[:])
            dst = dst_bf16.bitcast(F32).rearrange("p (c u) -> p c u", u=2)
            src = bank[:].rearrange("p u c -> p c u")
            if engine == "v":
                nc.vector.tensor_copy(out=dst, in_=src)
            else:
                nc.scalar.copy(out=dst, in_=src)

        w_grp, w_codes, w_scales = [], [], []
        for j in range(D // 2):
            w_grp.append(keep.tile([P, 2048], BF16, name="w_grp%d" % j, align_bytes=64))
            w_codes.append(keep.tile([P, 512], U32, name="w_codes%d" % j, align_bytes=64))
            w_scales.append(keep.tile([P, 512], U8, name="w_scales%d" % j, align_bytes=64))

        def quant_w(j):
            nc.vector.quantize_mx(out=w_codes[j][:].bitcast(FP8X4), scales=w_scales[j][:], in_=w_grp[j][:])

        for d in range(D):
            j, dd = d // 2, d % 2
            flip(w_sb[d][:].bitcast(F32), 0, w_grp[j][:, 1024 * dd : 1024 * (dd + 1)], "v" if d % 4 == 2 else "s")
            if dd == 1 and j >= 1:
                quant_w(j - 1)
        quant_w(D // 2 - 1)

        grp, codes, scales, res = {}, {}, {}, {}
        NU = 2 * NT

        def flip_x(u):
            i, h = u // 2, u % 2
            grp[u] = gpool.tile([P, 2048], BF16, name="x_grp", tag="x_grp", align_bytes=64)
            xw = x_sb[i][:].bitcast(F32)
            for j in range(2):
                on_vector = j == 1 and h == 0
                flip(xw, 1024 * h + 512 * j, grp[u][:, 1024 * j : 1024 * (j + 1)], "v" if on_vector else "s")

        def quant_x(u):
            codes[u] = gpool.tile([P, 4 * P], U32, name="x_codes", tag="x_codes", align_bytes=64)
            scales[u] = gpool.tile([P, 4 * P], U8, name="x_scales", tag="x_scales", align_bytes=64)
            nc.vector.quantize_mx(out=codes[u][:].bitcast(FP8X4), scales=scales[u][:], in_=grp[u][:])

        def multiply(u):
            i, h = u // 2, u % 2
            if h == 0:
                res[i] = opool.tile([P, D * O], F32, name="res", tag="res")
            for jj in range(2):
                j = 2 * h + jj
                acc = aps.tile([P, 2 * O], F32, name="acc", tag="acc")
                for dd in range(2):
                    dl = 2 * jj + dd
                    nc.tensor.matmul_mx(
                        out=acc[:, O * dd : O * (dd + 1)],
                        lhsT=codes[u][:, P * dl : P * (dl + 1)].bitcast(FP8X4),
                        lhsT_scale=scales[u][:, P * dl : P * (dl + 1)],
                        rhs=w_codes[j][:, O * dd : O * (dd + 1)].bitcast(FP8X4),
                        rhs_scale=w_scales[j][:, O * dd : O * (dd + 1)],
                        start=True,
                        stop=True,
                    )
                dst = res[i][:, 512 * j : 512 * (j + 1)]
                if jj == 0:
                    nc.vector.tensor_copy(out=dst, in_=acc[:])
                else:
                    nc.scalar.copy(out=dst, in_=acc[:])
            if h == 1:
                nc.sync.dma_start(out=out_v[:, i, :], in_=res[i][:])

        flip_x(0)
        flip_x(1)
        quant_x(0)
        for u in range(NU):
            if u + 1 < NU:
                quant_x(u + 1)
            if u + 2 < NU:
                flip_x(u + 2)
            multiply(u)
